import numpy as np
import ml_dtypes

BF16 = ml_dtypes.bfloat16


def bf(x):
    return np.asarray(x, np.float32).astype(BF16)


def f32(x):
    return np.asarray(x, np.float32)


def f64(x):
    return np.asarray(x).astype(np.float64)


def striped(idx):
    return np.tile(idx.reshape(-1, 16).T, (8, 1))


C, S, N, R, E = 128, 512, 128, 512, 512


def setup_inputs():
    return {"x": f32(np.random.standard_normal((C, S))), "sel": f32(np.random.uniform(0.0, 1.0, (C, N))), "mk": bf(np.random.standard_normal((C, R))), "shrink": f32(0.9 + 0.2 * np.random.uniform(0.0, 1.0, (R, 1))), "mv": bf(np.random.standard_normal((R, E))), "offs": striped(np.random.permutation(S)[:N])}


def reference(x, sel, mk, shrink, mv, offs):
    idx = offs[:16].T.reshape(-1)
    q = f64(x)[:, idx]
    u = q * f64(sel)
    bsq = np.sum(q * u, axis=0, keepdims=True)
    keys = np.concatenate([f64(mk) * f64(mk), f64(mk)], axis=0)
    qs = np.concatenate([-f64(sel), 2.0 * u], axis=0)
    sim = (keys.T @ qs - bsq) * f64(shrink) / np.sqrt(C)
    ex = np.exp(sim - sim.max(axis=0, keepdims=True))
    aff = ex / ex.sum(axis=0, keepdims=True)
    return f64(mv).T @ aff

@@ -1,0 +1,123 @@
+import math
+
+import concourse.mybir as mybir
+from concourse.masks import make_identity
+
+FP32 = mybir.dt.float32
+BF16 = mybir.dt.bfloat16
+U16 = mybir.dt.uint16
+ALU = mybir.AluOpType
+FUNC = mybir.ActivationFunctionType
+AXIS = mybir.AxisListType
+
+P = 128
+C, S, N, R, E = 128, 512, 128, 512, 512
+R_BLOCKS = R // P
+E_BLOCKS = E // P
+HALF_BLOCKS = R_BLOCKS // 2
+PSUM_BANKS = 8
+INV_SQRT_C = 1.0 / math.sqrt(C)
+
+FLOPS = 2 * (2 * C) * R * N + 2 * C * N + 2 * R * E * N
+
+
+def tile_vidsam_kernel(tc, x, sel, mk, shrink, mv, offs, out):
+    nc = tc.nc
+    with (
+        tc.tile_pool(name="held", bufs=1) as held,
+        tc.tile_pool(name="work", bufs=1) as work,
+        tc.tile_pool(name="staged", bufs=E_BLOCKS) as staged,
+        tc.psum_pool(name="banks", bufs=PSUM_BANKS) as banks,
+    ):
+        offsets = held.tile([P, N // 16], U16, name="offsets")
+        nc.sync.dma_start(offsets[:], offs)
+        x_sb = held.tile([C, S], FP32, name="x_sb")
+        nc.sync.dma_start(x_sb[:], x)
+        mk_sb = held.tile([C, R], BF16, name="mk_sb")
+        nc.scalar.dma_start(mk_sb[:], mk)
+        sel_sb = held.tile([C, N], FP32, name="sel_sb")
+        nc.scalar.dma_start(sel_sb[:], sel)
+        shrink_rows = held.tile([P, R], FP32, name="shrink_rows")
+        nc.sync.dma_start(shrink_rows[:], shrink.rearrange("r one -> (r one)").partition_broadcast(P))
+        mv_sb = held.tile([P, R_BLOCKS, E], BF16, name="mv_sb")
+        nc.sync.dma_start(mv_sb[:], mv.rearrange("(b p) e -> p b e", p=P))
+
+        identity = held.tile([P, P], BF16, name="identity")
+        make_identity(nc, identity[:])
+        identity_f32 = held.tile([P, P], FP32, name="identity_f32")
+        make_identity(nc, identity_f32[:])
+        ones = held.tile([C, 1], BF16, name="ones")
+        nc.gpsimd.memset(ones[:], 1.0)
+        warm = held.tile([P, 1], FP32, name="warm")
+        nc.vector.memset(warm[:], 0.0)
+        nc.scalar.activation(warm[:], warm[:], FUNC.Exp)
+
+        mk_sq = work.tile([C, R], BF16, name="mk_sq")
+        nc.vector.tensor_tensor(mk_sq[:], mk_sb[:], mk_sb[:], ALU.mult)
+        sel_bf = work.tile([C, N], BF16, name="sel_bf")
+        nc.vector.tensor_copy(sel_bf[:], sel_sb[:])
+
+        u = work.tile([C, N], FP32, name="u")
+        nc.vector.tensor_tensor(u[:], x_sb[:].indirect(offsets[:]), sel_sb[:], ALU.mult)
+        u_minus2 = work.tile([C, N], BF16, name="u_minus2")
+        nc.vector.tensor_scalar_mul(u_minus2[:], u[:], -2.0)
+        xu = work.tile([C, N], FP32, name="xu")
+        nc.vector.tensor_tensor(xu[:], x_sb[:].indirect(offsets[:]), u[:], ALU.mult)
+        xu_bf = work.tile([C, N], BF16, name="xu_bf")
+        nc.vector.tensor_copy(xu_bf[:], xu[:])
+
+        cross = banks.tile([N, R], FP32, name="cross", tag="bank")
+        nc.tensor.matmul(cross[:], sel_bf[:], mk_sq[:], start=True, stop=False)
+        nc.tensor.matmul(cross[:], u_minus2[:], mk_sb[:], start=False, stop=True)
+        bsq = banks.tile([N, 1], FP32, name="bsq", tag="bank")
+        nc.tensor.matmul(bsq[:], xu_bf[:], ones[:], start=True, stop=True)
+
+        dist = work.tile([N, R], FP32, name="dist")
+        nc.vector.scalar_tensor_tensor(dist[:], cross[:], bsq[:], shrink_rows[:], ALU.add, ALU.mult)
+
+        shifted = [banks.tile([P, N], FP32, name="shifted%d" % b, tag="bank") for b in range(R_BLOCKS)]
+        for b in range(R_BLOCKS):
+            nc.tensor.matmul(
+                shifted[b][:], dist[:, b * P : (b + 1) * P], identity_f32[:], is_transpose=True, start=True, stop=False
+            )
+
+        minus_smallest = work.tile([N, 1], BF16, name="minus_smallest")
+        with nc.allow_low_precision(reason="the shift of a softmax need not be the exact minimum"):
+            nc.vector.tensor_reduce(minus_smallest[:], dist[:], AXIS.X, ALU.min, negate=True)
+        for b in range(R_BLOCKS):
+            nc.tensor.matmul(shifted[b][:], minus_smallest[:].to_broadcast([N, P]), identity[:], start=False, stop=True)
+
+        shift = work.tile([N, 1], FP32, name="shift")
+        nc.scalar.mul(shift[:], minus_smallest[:], -INV_SQRT_C)
+        expo = work.tile([N, R], BF16, name="expo")
+        total = work.tile([N, 1], FP32, name="total")
+        nc.scalar.activation(expo[:], dist[:], FUNC.Exp, bias=shift[:], scale=-INV_SQRT_C, accum_out=total[:])
+
+        inv_total = work.tile([N, 1], FP32, name="inv_total")
+        nc.vector.reciprocal(inv_total[:], total[:])
+        inv_cols = work.tile([N, P], FP32, name="inv_cols")
+        nc.vector.tensor_copy(inv_cols[:], inv_total[:].to_broadcast([N, P]))
+
+        expo_t = work.tile([P, R_BLOCKS, N], BF16, name="expo_t")
+        for b in range(R_BLOCKS):
+            nc.scalar.activation(expo_t[:, b, :], shifted[b][:], FUNC.Exp, scale=-INV_SQRT_C)
+
+        acc = [banks.tile([P, N], FP32, name="acc%d" % e, tag="bank") for e in range(E_BLOCKS)]
+        inv_rows_ps = banks.tile([P, N], FP32, name="inv_rows_ps", tag="bank")
+        for b in range(HALF_BLOCKS):
+            for e in range(E_BLOCKS):
+                nc.tensor.matmul(acc[e][:], mv_sb[:, b, e * P : (e + 1) * P], expo_t[:, b, :], start=(b == 0), stop=False)
+            if b == 0:
+                nc.tensor.transpose(inv_rows_ps[:], inv_cols[:], identity_f32[:])
+        inv_rows = work.tile([P, N], FP32, name="inv_rows")
+        nc.vector.tensor_copy(inv_rows[:], inv_rows_ps[:])
+
+        for e in range(E_BLOCKS):
+            for b in range(HALF_BLOCKS, R_BLOCKS):
+                nc.tensor.matmul(
+                    acc[e][:], mv_sb[:, b, e * P : (e + 1) * P], expo_t[:, b, :], start=False, stop=(b == R_BLOCKS - 1)
+                )
+            block = staged.tile([P, N], FP32, name="block")
+            nc.vector.tensor_tensor(block[:], acc[e][:], inv_rows[:], ALU.mult)
+            queue = nc.sync if e % 2 == 0 else nc.scalar
+            queue.dma_start(out[e * P : (e + 1) * P, :], block[:])

@@ -37,8 +37,8 @@ def tile_vidsam_kernel(tc, x, sel, mk, shrink, mv, offs, out):
         nc.scalar.dma_start(mk_sb[:], mk)
         sel_sb = held.tile([C, N], FP32, name="sel_sb")
         nc.scalar.dma_start(sel_sb[:], sel)
-        shrink_rows = held.tile([P, R], FP32, name="shrink_rows")
-        nc.sync.dma_start(shrink_rows[:], shrink.rearrange("r one -> (r one)").partition_broadcast(P))
+        shrink_cols = held.tile([P, R_BLOCKS], FP32, name="shrink_cols")
+        nc.sync.dma_start(shrink_cols[:], shrink.rearrange("(p b) one -> p (b one)", b=R_BLOCKS))
         mv_sb = held.tile([P, R_BLOCKS, E], BF16, name="mv_sb")
         nc.sync.dma_start(mv_sb[:], mv.rearrange("(b p) e -> p b e", p=P))
 
@@ -51,6 +51,13 @@ def tile_vidsam_kernel(tc, x, sel, mk, shrink, mv, offs, out):
         warm = held.tile([P, 1], FP32, name="warm")
         nc.vector.memset(warm[:], 0.0)
         nc.scalar.activation(warm[:], warm[:], FUNC.Exp)
+
+        shrink_ps = banks.tile([P, R], FP32, name="shrink_ps", tag="bank")
+        shrink_by_col = shrink_ps[:].rearrange("q (p b) -> q b p", b=R_BLOCKS)
+        for b in range(R_BLOCKS):
+            nc.tensor.transpose(shrink_by_col[:, b, :], shrink_cols[:, b : b + 1].to_broadcast([P, P]), identity_f32[:])
+        shrink_rows = held.tile([P, R], FP32, name="shrink_rows")
+        nc.scalar.copy(shrink_rows[:], shrink_ps[:])
 
         mk_sq = work.tile([C, R], BF16, name="mk_sq")
         nc.vector.tensor_tensor(mk_sq[:], mk_sb[:], mk_sb[:], ALU.mult)

@@ -56,8 +56,8 @@ def tile_vidsam_kernel(tc, x, sel, mk, shrink, mv, offs, out):
         shrink_by_col = shrink_ps[:].rearrange("q (p b) -> q b p", b=R_BLOCKS)
         for b in range(R_BLOCKS):
             nc.tensor.transpose(shrink_by_col[:, b, :], shrink_cols[:, b : b + 1].to_broadcast([P, P]), identity_f32[:])
-        shrink_rows = held.tile([P, R], FP32, name="shrink_rows")
-        nc.scalar.copy(shrink_rows[:], shrink_ps[:])
+        minus_scale = held.tile([P, R], FP32, name="minus_scale")
+        nc.scalar.mul(minus_scale[:], shrink_ps[:], -INV_SQRT_C)
 
         mk_sq = work.tile([C, R], BF16, name="mk_sq")
         nc.vector.tensor_tensor(mk_sq[:], mk_sb[:], mk_sb[:], ALU.mult)
@@ -79,35 +79,31 @@ def tile_vidsam_kernel(tc, x, sel, mk, shrink, mv, offs, out):
         bsq = banks.tile([N, 1], FP32, name="bsq", tag="bank")
         nc.tensor.matmul(bsq[:], xu_bf[:], ones[:], start=True, stop=True)
 
-        dist = work.tile([N, R], FP32, name="dist")
-        nc.vector.scalar_tensor_tensor(dist[:], cross[:], bsq[:], shrink_rows[:], ALU.add, ALU.mult)
+        sim = work.tile([N, R], FP32, name="sim")
+        nc.vector.scalar_tensor_tensor(sim[:], cross[:], bsq[:], minus_scale[:], ALU.add, ALU.mult)
 
         shifted = [banks.tile([P, N], FP32, name="shifted%d" % b, tag="bank") for b in range(R_BLOCKS)]
         for b in range(R_BLOCKS):
             nc.tensor.matmul(
-                shifted[b][:], dist[:, b * P : (b + 1) * P], identity_f32[:], is_transpose=True, start=True, stop=False
+                shifted[b][:], sim[:, b * P : (b + 1) * P], identity_f32[:], is_transpose=True, start=True, stop=False
             )
 
-        minus_smallest = work.tile([N, 1], BF16, name="minus_smallest")
-        with nc.allow_low_precision(reason="the shift of a softmax need not be the exact minimum"):
-            nc.vector.tensor_reduce(minus_smallest[:], dist[:], AXIS.X, ALU.min, negate=True)
+        minus_largest = work.tile([N, 1], BF16, name="minus_largest")
+        with nc.allow_low_precision(reason="the shift of a softmax need not be the exact maximum"):
+            nc.vector.tensor_reduce(minus_largest[:], sim[:], AXIS.X, ALU.max, negate=True)
         for b in range(R_BLOCKS):
-            nc.tensor.matmul(shifted[b][:], minus_smallest[:].to_broadcast([N, P]), identity[:], start=False, stop=True)
+            nc.tensor.matmul(shifted[b][:], minus_largest[:].to_broadcast([N, P]), identity[:], start=False, stop=True)
 
-        shift = work.tile([N, 1], FP32, name="shift")
-        nc.scalar.mul(shift[:], minus_smallest[:], -INV_SQRT_C)
         expo = work.tile([N, R], BF16, name="expo")
         total = work.tile([N, 1], FP32, name="total")
-        nc.scalar.activation(expo[:], dist[:], FUNC.Exp, bias=shift[:], scale=-INV_SQRT_C, accum_out=total[:])
+        nc.scalar.activation(expo[:], sim[:], FUNC.Exp, bias=minus_largest[:], accum_out=total[:])
 
         inv_total = work.tile([N, 1], FP32, name="inv_total")
         nc.vector.reciprocal(inv_total[:], total[:])
-        inv_cols = work.tile([N, P], FP32, name="inv_cols")
-        nc.vector.tensor_copy(inv_cols[:], inv_total[:].to_broadcast([N, P]))
 
         expo_t = work.tile([P, R_BLOCKS, N], BF16, name="expo_t")
         for b in range(R_BLOCKS):
-            nc.scalar.activation(expo_t[:, b, :], shifted[b][:], FUNC.Exp, scale=-INV_SQRT_C)
+            nc.scalar.activation(expo_t[:, b, :], shifted[b][:], FUNC.Exp)
 
         acc = [banks.tile([P, N], FP32, name="acc%d" % e, tag="bank") for e in range(E_BLOCKS)]
         inv_rows_ps = banks.tile([P, N], FP32, name="inv_rows_ps", tag="bank")
@@ -115,7 +111,7 @@ def tile_vidsam_kernel(tc, x, sel, mk, shrink, mv, offs, out):
             for e in range(E_BLOCKS):
                 nc.tensor.matmul(acc[e][:], mv_sb[:, b, e * P : (e + 1) * P], expo_t[:, b, :], start=(b == 0), stop=False)
             if b == 0:
-                nc.tensor.transpose(inv_rows_ps[:], inv_cols[:], identity_f32[:])
+                nc.tensor.transpose(inv_rows_ps[:], inv_total[:].to_broadcast([N, P]), identity_f32[:])
         inv_rows = work.tile([P, N], FP32, name="inv_rows")
         nc.vector.tensor_copy(inv_rows[:], inv_rows_ps[:])
 

@@ -15,6 +15,7 @@ C, S, N, R, E = 128, 512, 128, 512, 512
 R_BLOCKS = R // P
 E_BLOCKS = E // P
 HALF_BLOCKS = R_BLOCKS // 2
+HALF_R = R // 2
 PSUM_BANKS = 8
 INV_SQRT_C = 1.0 / math.sqrt(C)
 
@@ -80,12 +81,19 @@ def tile_vidsam_kernel(tc, x, sel, mk, shrink, mv, offs, out):
         nc.tensor.matmul(bsq[:], xu_bf[:], ones[:], start=True, stop=True)
 
         sim = work.tile([N, R], FP32, name="sim")
-        nc.vector.scalar_tensor_tensor(sim[:], cross[:], bsq[:], minus_scale[:], ALU.add, ALU.mult)
+        for half in range(2):
+            cols = slice(half * HALF_R, (half + 1) * HALF_R)
+            nc.vector.scalar_tensor_tensor(sim[:, cols], cross[:, cols], bsq[:], minus_scale[:, cols], ALU.add, ALU.mult)
 
         shifted = [banks.tile([P, N], FP32, name="shifted%d" % b, tag="bank") for b in range(R_BLOCKS)]
         for b in range(R_BLOCKS):
             nc.tensor.matmul(
-                shifted[b][:], sim[:, b * P : (b + 1) * P], identity_f32[:], is_transpose=True, start=True, stop=False
+                shifted[b][:],
+                sim[:, b * P : (b + 1) * P],
+                identity_f32[:],
+                is_transpose=(b >= HALF_BLOCKS),
+                start=True,
+                stop=False,
             )
 
         minus_largest = work.tile([N, 1], BF16, name="minus_largest")

@@ -30,10 +30,10 @@ def tile_vidsam_kernel(tc, x, sel, mk, shrink, mv, offs, out):
         tc.tile_pool(name="staged", bufs=E_BLOCKS) as staged,
         tc.psum_pool(name="banks", bufs=PSUM_BANKS) as banks,
     ):
-        offsets = held.tile([P, N // 16], U16, name="offsets")
-        nc.sync.dma_start(offsets[:], offs)
         x_sb = held.tile([C, S], FP32, name="x_sb")
         nc.sync.dma_start(x_sb[:], x)
+        offsets = held.tile([P, N // 16], U16, name="offsets")
+        nc.sync.dma_start(offsets[:], offs)
         mk_sb = held.tile([C, R], BF16, name="mk_sb")
         nc.scalar.dma_start(mk_sb[:], mk)
         sel_sb = held.tile([C, N], FP32, name="sel_sb")
@@ -58,7 +58,9 @@ def tile_vidsam_kernel(tc, x, sel, mk, shrink, mv, offs, out):
         for b in range(R_BLOCKS):
             nc.tensor.transpose(shrink_by_col[:, b, :], shrink_cols[:, b : b + 1].to_broadcast([P, P]), identity_f32[:])
         minus_scale = held.tile([P, R], FP32, name="minus_scale")
-        nc.scalar.mul(minus_scale[:], shrink_ps[:], -INV_SQRT_C)
+        for half in range(2):
+            cols = slice(half * HALF_R, (half + 1) * HALF_R)
+            nc.scalar.mul(minus_scale[:, cols], shrink_ps[:, cols], -INV_SQRT_C)
 
         mk_sq = work.tile([C, R], BF16, name="mk_sq")
         nc.vector.tensor_tensor(mk_sq[:], mk_sb[:], mk_sb[:], ALU.mult)
@@ -86,21 +88,19 @@ def tile_vidsam_kernel(tc, x, sel, mk, shrink, mv, offs, out):
             nc.vector.scalar_tensor_tensor(sim[:, cols], cross[:, cols], bsq[:], minus_scale[:, cols], ALU.add, ALU.mult)
 
         shifted = [banks.tile([P, N], FP32, name="shifted%d" % b, tag="bank") for b in range(R_BLOCKS)]
-        for b in range(R_BLOCKS):
-            nc.tensor.matmul(
-                shifted[b][:],
-                sim[:, b * P : (b + 1) * P],
-                identity_f32[:],
-                is_transpose=(b >= HALF_BLOCKS),
-                start=True,
-                stop=False,
-            )
+        for b in range(HALF_BLOCKS):
+            nc.tensor.matmul(shifted[b][:], sim[:, b * P : (b + 1) * P], identity_f32[:], start=True, stop=False)
 
         minus_largest = work.tile([N, 1], BF16, name="minus_largest")
         with nc.allow_low_precision(reason="the shift of a softmax need not be the exact maximum"):
             nc.vector.tensor_reduce(minus_largest[:], sim[:], AXIS.X, ALU.max, negate=True)
-        for b in range(R_BLOCKS):
+        for b in range(HALF_BLOCKS):
             nc.tensor.matmul(shifted[b][:], minus_largest[:].to_broadcast([N, P]), identity[:], start=False, stop=True)
+        for b in range(HALF_BLOCKS, R_BLOCKS):
+            nc.tensor.matmul(shifted[b][:], minus_largest[:].to_broadcast([N, P]), identity[:], start=True, stop=False)
+            nc.tensor.matmul(
+                shifted[b][:], sim[:, b * P : (b + 1) * P], identity_f32[:], is_transpose=True, start=False, stop=True
+            )
 
         expo = work.tile([N, R], BF16, name="expo")
         total = work.tile([N, 1], FP32, name="total")

@@ -32,14 +32,14 @@ def tile_vidsam_kernel(tc, x, sel, mk, shrink, mv, offs, out):
     ):
         x_sb = held.tile([C, S], FP32, name="x_sb")
         nc.sync.dma_start(x_sb[:], x)
-        offsets = held.tile([P, N // 16], U16, name="offsets")
-        nc.sync.dma_start(offsets[:], offs)
         mk_sb = held.tile([C, R], BF16, name="mk_sb")
         nc.scalar.dma_start(mk_sb[:], mk)
-        sel_sb = held.tile([C, N], FP32, name="sel_sb")
-        nc.scalar.dma_start(sel_sb[:], sel)
         shrink_cols = held.tile([P, R_BLOCKS], FP32, name="shrink_cols")
         nc.sync.dma_start(shrink_cols[:], shrink.rearrange("(p b) one -> p (b one)", b=R_BLOCKS))
+        sel_sb = held.tile([C, N], FP32, name="sel_sb")
+        nc.scalar.dma_start(sel_sb[:], sel)
+        offsets = held.tile([P, N // 16], U16, name="offsets")
+        nc.sync.dma_start(offsets[:], offs)
         mv_sb = held.tile([P, R_BLOCKS, E], BF16, name="mv_sb")
         nc.sync.dma_start(mv_sb[:], mv.rearrange("(b p) e -> p b e", p=P))
 

import math

import concourse.mybir as mybir
from concourse.masks import make_identity

FP32 = mybir.dt.float32
BF16 = mybir.dt.bfloat16
U16 = mybir.dt.uint16
ALU = mybir.AluOpType
FUNC = mybir.ActivationFunctionType
AXIS = mybir.AxisListType

P = 128
C, S, N, R, E = 128, 512, 128, 512, 512
R_BLOCKS = R // P
E_BLOCKS = E // P
HALF_BLOCKS = R_BLOCKS // 2
HALF_R = R // 2
PSUM_BANKS = 8
INV_SQRT_C = 1.0 / math.sqrt(C)

FLOPS = 2 * (2 * C) * R * N + 2 * C * N + 2 * R * E * N


def tile_vidsam_kernel(tc, x, sel, mk, shrink, mv, offs, out):
    nc = tc.nc
    with (
        tc.tile_pool(name="held", bufs=1) as held,
        tc.tile_pool(name="work", bufs=1) as work,
        tc.tile_pool(name="staged", bufs=E_BLOCKS) as staged,
        tc.psum_pool(name="banks", bufs=PSUM_BANKS) as banks,
    ):
        x_sb = held.tile([C, S], FP32, name="x_sb")
        nc.sync.dma_start(x_sb[:], x)
        mk_sb = held.tile([C, R], BF16, name="mk_sb")
        nc.scalar.dma_start(mk_sb[:], mk)
        shrink_cols = held.tile([P, R_BLOCKS], FP32, name="shrink_cols")
        nc.sync.dma_start(shrink_cols[:], shrink.rearrange("(p b) one -> p (b one)", b=R_BLOCKS))
        sel_sb = held.tile([C, N], FP32, name="sel_sb")
        nc.scalar.dma_start(sel_sb[:], sel)
        offsets = held.tile([P, N // 16], U16, name="offsets")
        nc.sync.dma_start(offsets[:], offs)
        mv_sb = held.tile([P, R_BLOCKS, E], BF16, name="mv_sb")
        nc.sync.dma_start(mv_sb[:], mv.rearrange("(b p) e -> p b e", p=P))

        identity = held.tile([P, P], BF16, name="identity")
        make_identity(nc, identity[:])
        identity_f32 = held.tile([P, P], FP32, name="identity_f32")
        make_identity(nc, identity_f32[:])
        ones = held.tile([C, 1], BF16, name="ones")
        nc.gpsimd.memset(ones[:], 1.0)
        warm = held.tile([P, 1], FP32, name="warm")
        nc.vector.memset(warm[:], 0.0)
        nc.scalar.activation(warm[:], warm[:], FUNC.Exp)

        shrink_ps = banks.tile([P, R], FP32, name="shrink_ps", tag="bank")
        shrink_by_col = shrink_ps[:].rearrange("q (p b) -> q b p", b=R_BLOCKS)
        for b in range(R_BLOCKS):
            nc.tensor.transpose(shrink_by_col[:, b, :], shrink_cols[:, b : b + 1].to_broadcast([P, P]), identity_f32[:])
        minus_scale = held.tile([P, R], FP32, name="minus_scale")
        for half in range(2):
            cols = slice(half * HALF_R, (half + 1) * HALF_R)
            nc.scalar.mul(minus_scale[:, cols], shrink_ps[:, cols], -INV_SQRT_C)

        mk_sq = work.tile([C, R], BF16, name="mk_sq")
        nc.vector.tensor_tensor(mk_sq[:], mk_sb[:], mk_sb[:], ALU.mult)
        sel_bf = work.tile([C, N], BF16, name="sel_bf")
        nc.vector.tensor_copy(sel_bf[:], sel_sb[:])

        u = work.tile([C, N], FP32, name="u")
        nc.vector.tensor_tensor(u[:], x_sb[:].indirect(offsets[:]), sel_sb[:], ALU.mult)
        u_minus2 = work.tile([C, N], BF16, name="u_minus2")
        nc.vector.tensor_scalar_mul(u_minus2[:], u[:], -2.0)
        xu = work.tile([C, N], FP32, name="xu")
        nc.vector.tensor_tensor(xu[:], x_sb[:].indirect(offsets[:]), u[:], ALU.mult)
        xu_bf = work.tile([C, N], BF16, name="xu_bf")
        nc.vector.tensor_copy(xu_bf[:], xu[:])

        cross = banks.tile([N, R], FP32, name="cross", tag="bank")
        nc.tensor.matmul(cross[:], sel_bf[:], mk_sq[:], start=True, stop=False)
        nc.tensor.matmul(cross[:], u_minus2[:], mk_sb[:], start=False, stop=True)
        bsq = banks.tile([N, 1], FP32, name="bsq", tag="bank")
        nc.tensor.matmul(bsq[:], xu_bf[:], ones[:], start=True, stop=True)

        sim = work.tile([N, R], FP32, name="sim")
        for half in range(2):
            cols = slice(half * HALF_R, (half + 1) * HALF_R)
            nc.vector.scalar_tensor_tensor(sim[:, cols], cross[:, cols], bsq[:], minus_scale[:, cols], ALU.add, ALU.mult)

        shifted = [banks.tile([P, N], FP32, name="shifted%d" % b, tag="bank") for b in range(R_BLOCKS)]
        for b in range(HALF_BLOCKS):
            nc.tensor.matmul(shifted[b][:], sim[:, b * P : (b + 1) * P], identity_f32[:], start=True, stop=False)

        minus_largest = work.tile([N, 1], BF16, name="minus_largest")
        with nc.allow_low_precision(reason="the shift of a softmax need not be the exact maximum"):
            nc.vector.tensor_reduce(minus_largest[:], sim[:], AXIS.X, ALU.max, negate=True)
        for b in range(HALF_BLOCKS):
            nc.tensor.matmul(shifted[b][:], minus_largest[:].to_broadcast([N, P]), identity[:], start=False, stop=True)
        for b in range(HALF_BLOCKS, R_BLOCKS):
            nc.tensor.matmul(shifted[b][:], minus_largest[:].to_broadcast([N, P]), identity[:], start=True, stop=False)
            nc.tensor.matmul(
                shifted[b][:], sim[:, b * P : (b + 1) * P], identity_f32[:], is_transpose=True, start=False, stop=True
            )

        expo = work.tile([N, R], BF16, name="expo")
        total = work.tile([N, 1], FP32, name="total")
        nc.scalar.activation(expo[:], sim[:], FUNC.Exp, bias=minus_largest[:], accum_out=total[:])

        inv_total = work.tile([N, 1], FP32, name="inv_total")
        nc.vector.reciprocal(inv_total[:], total[:])

        expo_t = work.tile([P, R_BLOCKS, N], BF16, name="expo_t")
        for b in range(R_BLOCKS):
            nc.scalar.activation(expo_t[:, b, :], shifted[b][:], FUNC.Exp)

        acc = [banks.tile([P, N], FP32, name="acc%d" % e, tag="bank") for e in range(E_BLOCKS)]
        inv_rows_ps = banks.tile([P, N], FP32, name="inv_rows_ps", tag="bank")
        for b in range(HALF_BLOCKS):
            for e in range(E_BLOCKS):
                nc.tensor.matmul(acc[e][:], mv_sb[:, b, e * P : (e + 1) * P], expo_t[:, b, :], start=(b == 0), stop=False)
            if b == 0:
                nc.tensor.transpose(inv_rows_ps[:], inv_total[:].to_broadcast([N, P]), identity_f32[:])
        inv_rows = work.tile([P, N], FP32, name="inv_rows")
        nc.vector.tensor_copy(inv_rows[:], inv_rows_ps[:])

        for e in range(E_BLOCKS):
            for b in range(HALF_BLOCKS, R_BLOCKS):
                nc.tensor.matmul(
                    acc[e][:], mv_sb[:, b, e * P : (e + 1) * P], expo_t[:, b, :], start=False, stop=(b == R_BLOCKS - 1)
                )
            block = staged.tile([P, N], FP32, name="block")
            nc.vector.tensor_tensor(block[:], acc[e][:], inv_rows[:], ALU.mult)
            queue = nc.sync if e % 2 == 0 else nc.scalar
            queue.dma_start(out[e * P : (e + 1) * P, :], block[:])
